import numpy as np
import ml_dtypes

BF16 = ml_dtypes.bfloat16


def bf(x):
    return np.asarray(x, np.float32).astype(BF16)


def f32(x):
    return np.asarray(x, np.float32)


def f64(x):
    return np.asarray(x).astype(np.float64)


def striped(idx):
    return np.tile(idx.reshape(-1, 16).T, (8, 1))


H, D, S, N = 2, 128, 256, 128


def setup_inputs():
    return {"base": f32(0.1 * np.random.standard_normal((H * S, S))), "query": bf(2.0 * np.random.standard_normal((H * D, N))), "key_emb": bf(np.random.standard_normal((H * D, S))), "offs": striped(np.random.permutation(S)[:N])}


def reference(base, query, key_emb, offs):
    idx = offs[:16].T.reshape(-1)
    qh = f64(query).reshape(H, D, N)
    kh = f64(key_emb).reshape(H, D, S)
    e = np.exp(np.einsum("hdt,hdn->htn", kh, qh) / np.sqrt(D))
    r = 1.0 / e.sum(axis=1, keepdims=True)
    out = f64(base).copy()
    out[:, idx] = (e * r).reshape(H * S, N)
    return out

@@ -1,0 +1,80 @@
+import math
+
+import concourse.mybir as mybir
+from concourse.masks import make_identity
+
+HEADS = 2
+FEATURES = 128
+CONCEPTS = 256
+PLACES = 256
+QUESTIONS = 128
+P = 128
+BLOCKS = CONCEPTS // P
+SCALE = 1.0 / math.sqrt(FEATURES)
+
+FLOPS = 2 * HEADS * CONCEPTS * QUESTIONS * FEATURES
+
+F32 = mybir.dt.float32
+BF16 = mybir.dt.bfloat16
+U16 = mybir.dt.uint16
+MULT = mybir.AluOpType.mult
+EXP = mybir.ActivationFunctionType.Exp
+
+
+def tile_multiheadattention_kernel(tc, base, query, key_emb, offs, out):
+    nc = tc.nc
+    with (
+        tc.tile_pool(name="held", bufs=1) as held,
+        tc.psum_pool(name="psum_flipped", bufs=HEADS) as psum_flipped,
+        tc.psum_pool(name="psum_scores", bufs=HEADS * BLOCKS) as psum_scores,
+        tc.psum_pool(name="psum_sums", bufs=HEADS) as psum_sums,
+    ):
+        keys = []
+        questions = []
+        for h in range(HEADS):
+            key_h = held.tile([FEATURES, CONCEPTS], BF16, name=f"key{h}")
+            nc.sync.dma_start(key_h[:], key_emb[h * FEATURES : (h + 1) * FEATURES, :])
+            keys.append(key_h)
+            question_h = held.tile([FEATURES, QUESTIONS], BF16, name=f"question{h}")
+            nc.scalar.dma_start(question_h[:], query[h * FEATURES : (h + 1) * FEATURES, :])
+            questions.append(question_h)
+        offsets = held.tile([P, QUESTIONS // 16], U16, name="offsets")
+        nc.sync.dma_start(offsets[:], offs)
+        windows = []
+        for w in range(HEADS * BLOCKS):
+            window = held.tile([P, PLACES], F32, name=f"window{w}")
+            nc.sync.dma_start(window[:], base[w * P : (w + 1) * P, :])
+            windows.append(window)
+
+        identity = held.tile([P, P], F32, name="identity")
+        make_identity(nc, identity[:])
+        ones = held.tile([P, P], F32, name="ones")
+        nc.gpsimd.memset(ones[:], 1.0)
+
+        for h in range(HEADS):
+            flipped = psum_flipped.tile([QUESTIONS, CONCEPTS], F32, name="flipped")
+            nc.tensor.matmul(flipped[:], questions[h][:], keys[h][:], start=True, stop=True)
+            largest = held.tile([QUESTIONS, 1], F32, name=f"largest{h}")
+            nc.vector.reduce_max(largest[:], flipped[:], axis=mybir.AxisListType.X)
+            shift = held.tile([QUESTIONS, QUESTIONS], F32, name=f"shift{h}")
+            nc.vector.tensor_scalar(shift[:], identity[:], largest[:], -1.0, MULT, MULT)
+
+            sums = psum_sums.tile([P, QUESTIONS], F32, name="sums")
+            exps = []
+            for b in range(BLOCKS):
+                scores = psum_scores.tile([P, QUESTIONS], F32, name="scores")
+                nc.tensor.matmul(
+                    scores[:], keys[h][:, b * P : (b + 1) * P], questions[h][:], start=True, stop=False
+                )
+                nc.tensor.matmul(scores[:], ones[:], shift[:], start=False, stop=True)
+                e = held.tile([P, QUESTIONS], F32, name=f"e{h}{b}")
+                nc.scalar.activation(e[:], scores[:], EXP, scale=SCALE)
+                nc.tensor.matmul(sums[:], ones[:], e[:], start=(b == 0), stop=(b == BLOCKS - 1))
+                exps.append(e)
+            r = held.tile([P, QUESTIONS], F32, name=f"r{h}")
+            nc.vector.reciprocal(r[:], sums[:])
+
+            for b in range(BLOCKS):
+                w = h * BLOCKS + b
+                nc.vector.tensor_tensor(windows[w][:].indirect(offsets[:]), exps[b][:], r[:], MULT)
+                nc.sync.dma_start(out[w * P : (w + 1) * P, :], windows[w][:])

@@ -25,9 +25,7 @@ def tile_multiheadattention_kernel(tc, base, query, key_emb, offs, out):
     nc = tc.nc
     with (
         tc.tile_pool(name="held", bufs=1) as held,
-        tc.psum_pool(name="psum_flipped", bufs=HEADS) as psum_flipped,
-        tc.psum_pool(name="psum_scores", bufs=HEADS * BLOCKS) as psum_scores,
-        tc.psum_pool(name="psum_sums", bufs=HEADS) as psum_sums,
+        tc.psum_pool(name="psum", bufs=1) as psum,
     ):
         keys = []
         questions = []
@@ -52,29 +50,37 @@ def tile_multiheadattention_kernel(tc, base, query, key_emb, offs, out):
         nc.gpsimd.memset(ones[:], 1.0)
 
         for h in range(HEADS):
-            flipped = psum_flipped.tile([QUESTIONS, CONCEPTS], F32, name="flipped")
-            nc.tensor.matmul(flipped[:], questions[h][:], keys[h][:], start=True, stop=True)
-            largest = held.tile([QUESTIONS, 1], F32, name=f"largest{h}")
-            nc.vector.reduce_max(largest[:], flipped[:], axis=mybir.AxisListType.X)
-            shift = held.tile([QUESTIONS, QUESTIONS], F32, name=f"shift{h}")
-            nc.vector.tensor_scalar(shift[:], identity[:], largest[:], -1.0, MULT, MULT)
+            scores = psum.tile([QUESTIONS, CONCEPTS], F32, name=f"scores{h}")
+            nc.tensor.matmul(scores[:], questions[h][:], keys[h][:], start=True, stop=True)
 
-            sums = psum_sums.tile([P, QUESTIONS], F32, name="sums")
-            exps = []
+            largest = held.tile([QUESTIONS, 1], F32, name=f"largest{h}")
+            nc.vector.reduce_max(largest[:], scores[:], axis=mybir.AxisListType.X)
+            bias = held.tile([QUESTIONS, 1], F32, name=f"bias{h}")
+            nc.vector.tensor_scalar(bias[:], largest[:], -SCALE, None, MULT)
+            e_by_question = held.tile([QUESTIONS, CONCEPTS], F32, name=f"e_by_question{h}")
+            total = held.tile([QUESTIONS, 1], F32, name=f"total{h}")
+            nc.scalar.activation(
+                e_by_question[:], scores[:], EXP, bias=bias[:], scale=SCALE, accum_out=total[:]
+            )
+
+            r_by_question = held.tile([QUESTIONS, 1], F32, name=f"r_by_question{h}")
+            nc.vector.reciprocal(r_by_question[:], total[:])
+            r_repeated = held.tile([QUESTIONS, P], F32, name=f"r_repeated{h}")
+            nc.vector.tensor_scalar(r_repeated[:], ones[:], r_by_question[:], None, MULT)
+
+            e_flipped = psum.tile([P, BLOCKS, QUESTIONS], F32, name=f"e_flipped{h}")
             for b in range(BLOCKS):
-                scores = psum_scores.tile([P, QUESTIONS], F32, name="scores")
-                nc.tensor.matmul(
-                    scores[:], keys[h][:, b * P : (b + 1) * P], questions[h][:], start=True, stop=False
+                nc.tensor.transpose(
+                    e_flipped[:, b, :], e_by_question[:, b * P : (b + 1) * P], identity[:]
                 )
-                nc.tensor.matmul(scores[:], ones[:], shift[:], start=False, stop=True)
-                e = held.tile([P, QUESTIONS], F32, name=f"e{h}{b}")
-                nc.scalar.activation(e[:], scores[:], EXP, scale=SCALE)
-                nc.tensor.matmul(sums[:], ones[:], e[:], start=(b == 0), stop=(b == BLOCKS - 1))
-                exps.append(e)
+            r_flipped = psum.tile([P, QUESTIONS], F32, name=f"r_flipped{h}")
+            nc.tensor.transpose(r_flipped[:], r_repeated[:], identity[:])
+            e = held.tile([P, BLOCKS, QUESTIONS], F32, name=f"e{h}")
+            nc.scalar.copy(e[:], e_flipped[:])
             r = held.tile([P, QUESTIONS], F32, name=f"r{h}")
-            nc.vector.reciprocal(r[:], sums[:])
+            nc.scalar.copy(r[:], r_flipped[:])
 
             for b in range(BLOCKS):
                 w = h * BLOCKS + b
-                nc.vector.tensor_tensor(windows[w][:].indirect(offsets[:]), exps[b][:], r[:], MULT)
+                nc.vector.tensor_tensor(windows[w][:].indirect(offsets[:]), e[:, b, :], r[:], MULT)
                 nc.sync.dma_start(out[w * P : (w + 1) * P, :], windows[w][:])

@@ -46,17 +46,16 @@ def tile_multiheadattention_kernel(tc, base, query, key_emb, offs, out):
 
         identity = held.tile([P, P], F32, name="identity")
         make_identity(nc, identity[:])
-        ones = held.tile([P, P], F32, name="ones")
-        nc.gpsimd.memset(ones[:], 1.0)
 
         for h in range(HEADS):
             scores = psum.tile([QUESTIONS, CONCEPTS], F32, name=f"scores{h}")
             nc.tensor.matmul(scores[:], questions[h][:], keys[h][:], start=True, stop=True)
 
-            largest = held.tile([QUESTIONS, 1], F32, name=f"largest{h}")
-            nc.vector.reduce_max(largest[:], scores[:], axis=mybir.AxisListType.X)
+            negated = held.tile([QUESTIONS, CONCEPTS], F32, name=f"negated{h}")
             bias = held.tile([QUESTIONS, 1], F32, name=f"bias{h}")
-            nc.vector.tensor_scalar(bias[:], largest[:], -SCALE, None, MULT)
+            nc.vector.tensor_scalar(
+                negated[:], scores[:], -SCALE, None, MULT, mybir.AluOpType.min, accum_out=bias[:]
+            )
             e_by_question = held.tile([QUESTIONS, CONCEPTS], F32, name=f"e_by_question{h}")
             total = held.tile([QUESTIONS, 1], F32, name=f"total{h}")
             nc.scalar.activation(
@@ -65,22 +64,21 @@ def tile_multiheadattention_kernel(tc, base, query, key_emb, offs, out):
 
             r_by_question = held.tile([QUESTIONS, 1], F32, name=f"r_by_question{h}")
             nc.vector.reciprocal(r_by_question[:], total[:])
-            r_repeated = held.tile([QUESTIONS, P], F32, name=f"r_repeated{h}")
-            nc.vector.tensor_scalar(r_repeated[:], ones[:], r_by_question[:], None, MULT)
 
-            e_flipped = psum.tile([P, BLOCKS, QUESTIONS], F32, name=f"e_flipped{h}")
+            copy_out = nc.vector.tensor_copy if h == 0 else nc.scalar.copy
+            e_blocks = []
             for b in range(BLOCKS):
-                nc.tensor.transpose(
-                    e_flipped[:, b, :], e_by_question[:, b * P : (b + 1) * P], identity[:]
-                )
+                e_flipped = psum.tile([P, QUESTIONS], F32, name=f"e_flipped{h}{b}")
+                nc.tensor.transpose(e_flipped[:], e_by_question[:, b * P : (b + 1) * P], identity[:])
+                e = held.tile([P, QUESTIONS], F32, name=f"e{h}{b}")
+                copy_out(e[:], e_flipped[:])
+                e_blocks.append(e)
             r_flipped = psum.tile([P, QUESTIONS], F32, name=f"r_flipped{h}")
-            nc.tensor.transpose(r_flipped[:], r_repeated[:], identity[:])
-            e = held.tile([P, BLOCKS, QUESTIONS], F32, name=f"e{h}")
-            nc.scalar.copy(e[:], e_flipped[:])
+            nc.tensor.transpose(r_flipped[:], r_by_question[:].to_broadcast([QUESTIONS, P]), identity[:])
             r = held.tile([P, QUESTIONS], F32, name=f"r{h}")
-            nc.scalar.copy(r[:], r_flipped[:])
+            copy_out(r[:], r_flipped[:])
 
             for b in range(BLOCKS):
                 w = h * BLOCKS + b
-                nc.vector.tensor_tensor(windows[w][:].indirect(offsets[:]), e[:, b, :], r[:], MULT)
+                nc.vector.tensor_tensor(windows[w][:].indirect(offsets[:]), e_blocks[b][:], r[:], MULT)
                 nc.sync.dma_start(out[w * P : (w + 1) * P, :], windows[w][:])

@@ -65,18 +65,20 @@ def tile_multiheadattention_kernel(tc, base, query, key_emb, offs, out):
             r_by_question = held.tile([QUESTIONS, 1], F32, name=f"r_by_question{h}")
             nc.vector.reciprocal(r_by_question[:], total[:])
 
-            copy_out = nc.vector.tensor_copy if h == 0 else nc.scalar.copy
-            e_blocks = []
-            for b in range(BLOCKS):
-                e_flipped = psum.tile([P, QUESTIONS], F32, name=f"e_flipped{h}{b}")
-                nc.tensor.transpose(e_flipped[:], e_by_question[:, b * P : (b + 1) * P], identity[:])
-                e = held.tile([P, QUESTIONS], F32, name=f"e{h}{b}")
-                copy_out(e[:], e_flipped[:])
-                e_blocks.append(e)
-            r_flipped = psum.tile([P, QUESTIONS], F32, name=f"r_flipped{h}")
-            nc.tensor.transpose(r_flipped[:], r_by_question[:].to_broadcast([QUESTIONS, P]), identity[:])
-            r = held.tile([P, QUESTIONS], F32, name=f"r{h}")
-            copy_out(r[:], r_flipped[:])
+            first_copy = nc.vector.tensor_copy if h == 0 else nc.scalar.copy
+            to_flip = [
+                ("e0", e_by_question[:, 0:P], first_copy),
+                ("r", r_by_question[:].to_broadcast([QUESTIONS, P]), first_copy),
+                ("e1", e_by_question[:, P : 2 * P], nc.scalar.copy),
+            ]
+            flipped = {}
+            for name, by_question, copy_out in to_flip:
+                in_psum = psum.tile([P, QUESTIONS], F32, name=f"{name}_psum{h}")
+                nc.tensor.transpose(in_psum[:], by_question, identity[:])
+                flipped[name] = held.tile([P, QUESTIONS], F32, name=f"{name}_{h}")
+                copy_out(flipped[name][:], in_psum[:])
+            e_blocks = [flipped["e0"], flipped["e1"]]
+            r = flipped["r"]
 
             for b in range(BLOCKS):
                 w = h * BLOCKS + b

@@ -48,13 +48,15 @@ def tile_multiheadattention_kernel(tc, base, query, key_emb, offs, out):
         make_identity(nc, identity[:])
 
         for h in range(HEADS):
+            rounded = psum.tile([QUESTIONS, CONCEPTS], BF16, name=f"rounded{h}", tag=f"rounded_then_r{h}")
+            nc.tensor.matmul(rounded[:], questions[h][:], keys[h][:], start=True, stop=True)
             scores = psum.tile([QUESTIONS, CONCEPTS], F32, name=f"scores{h}")
             nc.tensor.matmul(scores[:], questions[h][:], keys[h][:], start=True, stop=True)
 
-            negated = held.tile([QUESTIONS, CONCEPTS], F32, name=f"negated{h}")
+            negated = held.tile([QUESTIONS, CONCEPTS], BF16, name=f"negated{h}")
             bias = held.tile([QUESTIONS, 1], F32, name=f"bias{h}")
             nc.vector.tensor_scalar(
-                negated[:], scores[:], -SCALE, None, MULT, mybir.AluOpType.min, accum_out=bias[:]
+                negated[:], rounded[:], -SCALE, None, MULT, mybir.AluOpType.min, accum_out=bias[:]
             )
             e_by_question = held.tile([QUESTIONS, CONCEPTS], F32, name=f"e_by_question{h}")
             total = held.tile([QUESTIONS, 1], F32, name=f"total{h}")
@@ -73,7 +75,8 @@ def tile_multiheadattention_kernel(tc, base, query, key_emb, offs, out):
             ]
             flipped = {}
             for name, by_question, copy_out in to_flip:
-                in_psum = psum.tile([P, QUESTIONS], F32, name=f"{name}_psum{h}")
+                tag = f"rounded_then_r{h}" if name == "r" else f"{name}_psum{h}"
+                in_psum = psum.tile([P, QUESTIONS], F32, name=f"{name}_psum{h}", tag=tag)
                 nc.tensor.transpose(in_psum[:], by_question, identity[:])
                 flipped[name] = held.tile([P, QUESTIONS], F32, name=f"{name}_{h}")
                 copy_out(flipped[name][:], in_psum[:])

@@ -44,6 +44,11 @@ def tile_multiheadattention_kernel(tc, base, query, key_emb, offs, out):
             nc.sync.dma_start(window[:], base[w * P : (w + 1) * P, :])
             windows.append(window)
 
+        zero = held.tile([P, 1], F32, name="zero")
+        nc.vector.memset(zero[:], 0.0)
+        one = held.tile([P, 1], F32, name="one")
+        nc.scalar.activation(one[:], zero[:], EXP)
+
         identity = held.tile([P, P], F32, name="identity")
         make_identity(nc, identity[:])
 

@@ -1,7 +1,6 @@
 import math
 
 import concourse.mybir as mybir
-from concourse.masks import make_identity
 
 HEADS = 2
 FEATURES = 128
@@ -9,6 +8,7 @@ CONCEPTS = 256
 PLACES = 256
 QUESTIONS = 128
 P = 128
+SQUARE = 32
 BLOCKS = CONCEPTS // P
 SCALE = 1.0 / math.sqrt(FEATURES)
 
@@ -49,8 +49,19 @@ def tile_multiheadattention_kernel(tc, base, query, key_emb, offs, out):
         one = held.tile([P, 1], F32, name="one")
         nc.scalar.activation(one[:], zero[:], EXP)
 
+        ones = held.tile([P, SQUARE], F32, name="ones")
+        nc.vector.memset(ones[:], 1.0)
+        column = held.tile([P, SQUARE], F32, name="column", align_bytes=64)
+        nc.vector.tensor_tensor_scan(column[:], ones[:], ones[:], -1.0, MULT, mybir.AluOpType.add)
+        row = held.tile([P, SQUARE], F32, name="row", align_bytes=64)
+        nc.vector.transpose(row[:], column[:])
         identity = held.tile([P, P], F32, name="identity")
-        make_identity(nc, identity[:])
+        nc.vector.memset(identity[:], 0.0)
+        for start in range(0, P, SQUARE):
+            square = slice(start, start + SQUARE)
+            nc.vector.tensor_tensor(
+                identity[square, square], column[square, :], row[square, :], mybir.AluOpType.is_equal
+            )
 
         for h in range(HEADS):
             rounded = psum.tile([QUESTIONS, CONCEPTS], BF16, name=f"rounded{h}", tag=f"rounded_then_r{h}")

@@ -31,10 +31,10 @@ def tile_multiheadattention_kernel(tc, base, query, key_emb, offs, out):
         questions = []
         for h in range(HEADS):
             key_h = held.tile([FEATURES, CONCEPTS], BF16, name=f"key{h}")
-            nc.sync.dma_start(key_h[:], key_emb[h * FEATURES : (h + 1) * FEATURES, :])
+            nc.scalar.dma_start(key_h[:], key_emb[h * FEATURES : (h + 1) * FEATURES, :])
             keys.append(key_h)
             question_h = held.tile([FEATURES, QUESTIONS], BF16, name=f"question{h}")
-            nc.scalar.dma_start(question_h[:], query[h * FEATURES : (h + 1) * FEATURES, :])
+            nc.sync.dma_start(question_h[:], query[h * FEATURES : (h + 1) * FEATURES, :])
             questions.append(question_h)
         offsets = held.tile([P, QUESTIONS // 16], U16, name="offsets")
         nc.sync.dma_start(offsets[:], offs)

@@ -41,7 +41,11 @@ def tile_multiheadattention_kernel(tc, base, query, key_emb, offs, out):
         windows = []
         for w in range(HEADS * BLOCKS):
             window = held.tile([P, PLACES], F32, name=f"window{w}")
-            nc.sync.dma_start(window[:], base[w * P : (w + 1) * P, :])
+            rows = P if w == 0 else P // 2
+            for row in range(0, P, rows):
+                nc.sync.dma_start(
+                    window[row : row + rows, :], base[w * P + row : w * P + row + rows, :]
+                )
             windows.append(window)
 
         zero = held.tile([P, 1], F32, name="zero")

@@ -72,6 +72,9 @@ def tile_multiheadattention_kernel(tc, base, query, key_emb, offs, out):
             nc.tensor.matmul(rounded[:], questions[h][:], keys[h][:], start=True, stop=True)
             scores = psum.tile([QUESTIONS, CONCEPTS], F32, name=f"scores{h}")
             nc.tensor.matmul(scores[:], questions[h][:], keys[h][:], start=True, stop=True)
+            if h == 0:
+                seen = held.tile([QUESTIONS, 1], F32, name="seen")
+                nc.scalar.copy(seen[:], scores[:, 0:1])
 
             negated = held.tile([QUESTIONS, CONCEPTS], BF16, name=f"negated{h}")
             bias = held.tile([QUESTIONS, 1], F32, name=f"bias{h}")

@@ -98,7 +98,7 @@ def tile_multiheadattention_kernel(tc, base, query, key_emb, offs, out):
             ]
             flipped = {}
             for name, by_question, copy_out in to_flip:
-                tag = f"rounded_then_r{h}" if name == "r" else f"{name}_psum{h}"
+                tag = f"rounded_then_r{h}" if name == "r" else f"e_psum{h}"
                 in_psum = psum.tile([P, QUESTIONS], F32, name=f"{name}_psum{h}", tag=tag)
                 nc.tensor.transpose(in_psum[:], by_question, identity[:])
                 flipped[name] = held.tile([P, QUESTIONS], F32, name=f"{name}_{h}")

import math

import concourse.mybir as mybir

HEADS = 2
FEATURES = 128
CONCEPTS = 256
PLACES = 256
QUESTIONS = 128
P = 128
SQUARE = 32
BLOCKS = CONCEPTS // P
SCALE = 1.0 / math.sqrt(FEATURES)

FLOPS = 2 * HEADS * CONCEPTS * QUESTIONS * FEATURES

F32 = mybir.dt.float32
BF16 = mybir.dt.bfloat16
U16 = mybir.dt.uint16
MULT = mybir.AluOpType.mult
EXP = mybir.ActivationFunctionType.Exp


def tile_multiheadattention_kernel(tc, base, query, key_emb, offs, out):
    nc = tc.nc
    with (
        tc.tile_pool(name="held", bufs=1) as held,
        tc.psum_pool(name="psum", bufs=1) as psum,
    ):
        keys = []
        questions = []
        for h in range(HEADS):
            key_h = held.tile([FEATURES, CONCEPTS], BF16, name=f"key{h}")
            nc.scalar.dma_start(key_h[:], key_emb[h * FEATURES : (h + 1) * FEATURES, :])
            keys.append(key_h)
            question_h = held.tile([FEATURES, QUESTIONS], BF16, name=f"question{h}")
            nc.sync.dma_start(question_h[:], query[h * FEATURES : (h + 1) * FEATURES, :])
            questions.append(question_h)
        offsets = held.tile([P, QUESTIONS // 16], U16, name="offsets")
        nc.sync.dma_start(offsets[:], offs)
        windows = []
        for w in range(HEADS * BLOCKS):
            window = held.tile([P, PLACES], F32, name=f"window{w}")
            rows = P if w == 0 else P // 2
            for row in range(0, P, rows):
                nc.sync.dma_start(
                    window[row : row + rows, :], base[w * P + row : w * P + row + rows, :]
                )
            windows.append(window)

        zero = held.tile([P, 1], F32, name="zero")
        nc.vector.memset(zero[:], 0.0)
        one = held.tile([P, 1], F32, name="one")
        nc.scalar.activation(one[:], zero[:], EXP)

        ones = held.tile([P, SQUARE], F32, name="ones")
        nc.vector.memset(ones[:], 1.0)
        column = held.tile([P, SQUARE], F32, name="column", align_bytes=64)
        nc.vector.tensor_tensor_scan(column[:], ones[:], ones[:], -1.0, MULT, mybir.AluOpType.add)
        row = held.tile([P, SQUARE], F32, name="row", align_bytes=64)
        nc.vector.transpose(row[:], column[:])
        identity = held.tile([P, P], F32, name="identity")
        nc.vector.memset(identity[:], 0.0)
        for start in range(0, P, SQUARE):
            square = slice(start, start + SQUARE)
            nc.vector.tensor_tensor(
                identity[square, square], column[square, :], row[square, :], mybir.AluOpType.is_equal
            )

        for h in range(HEADS):
            rounded = psum.tile([QUESTIONS, CONCEPTS], BF16, name=f"rounded{h}", tag=f"rounded_then_r{h}")
            nc.tensor.matmul(rounded[:], questions[h][:], keys[h][:], start=True, stop=True)
            scores = psum.tile([QUESTIONS, CONCEPTS], F32, name=f"scores{h}")
            nc.tensor.matmul(scores[:], questions[h][:], keys[h][:], start=True, stop=True)
            if h == 0:
                seen = held.tile([QUESTIONS, 1], F32, name="seen")
                nc.scalar.copy(seen[:], scores[:, 0:1])

            negated = held.tile([QUESTIONS, CONCEPTS], BF16, name=f"negated{h}")
            bias = held.tile([QUESTIONS, 1], F32, name=f"bias{h}")
            nc.vector.tensor_scalar(
                negated[:], rounded[:], -SCALE, None, MULT, mybir.AluOpType.min, accum_out=bias[:]
            )
            e_by_question = held.tile([QUESTIONS, CONCEPTS], F32, name=f"e_by_question{h}")
            total = held.tile([QUESTIONS, 1], F32, name=f"total{h}")
            nc.scalar.activation(
                e_by_question[:], scores[:], EXP, bias=bias[:], scale=SCALE, accum_out=total[:]
            )

            r_by_question = held.tile([QUESTIONS, 1], F32, name=f"r_by_question{h}")
            nc.vector.reciprocal(r_by_question[:], total[:])

            first_copy = nc.vector.tensor_copy if h == 0 else nc.scalar.copy
            to_flip = [
                ("e0", e_by_question[:, 0:P], first_copy),
                ("r", r_by_question[:].to_broadcast([QUESTIONS, P]), first_copy),
                ("e1", e_by_question[:, P : 2 * P], nc.scalar.copy),
            ]
            flipped = {}
            for name, by_question, copy_out in to_flip:
                tag = f"rounded_then_r{h}" if name == "r" else f"e_psum{h}"
                in_psum = psum.tile([P, QUESTIONS], F32, name=f"{name}_psum{h}", tag=tag)
                nc.tensor.transpose(in_psum[:], by_question, identity[:])
                flipped[name] = held.tile([P, QUESTIONS], F32, name=f"{name}_{h}")
                copy_out(flipped[name][:], in_psum[:])
            e_blocks = [flipped["e0"], flipped["e1"]]
            r = flipped["r"]

            for b in range(BLOCKS):
                w = h * BLOCKS + b
                nc.vector.tensor_tensor(windows[w][:].indirect(offsets[:]), e_blocks[b][:], r[:], MULT)
                nc.sync.dma_start(out[w * P : (w + 1) * P, :], windows[w][:])
